import numpy as np
import ml_dtypes


def mxq(x, axis, fmt="e4m3"):
    dtype, down = {"e4m3": (ml_dtypes.float8_e4m3fn, 7), "e5m2": (ml_dtypes.float8_e5m2, 14)}[fmt]
    v = np.moveaxis(np.asarray(x, np.float32).astype(ml_dtypes.bfloat16).astype(np.float64), axis, -1)
    blocks = v.reshape(v.shape[:-1] + (-1, 32))
    amax = np.abs(blocks).max(-1, keepdims=True)
    byte = np.maximum(np.where(amax > 0, np.frexp(amax)[1] - 1 + 127, 0) - down, 1)
    scale = np.exp2(byte - 127.0)
    codes = (blocks / scale).astype(np.float32).astype(dtype).astype(np.float64)
    return np.moveaxis((codes * scale).reshape(v.shape), -1, axis)


WIDE = False


def mx_kscale(k):
    if not WIDE:
        return np.ones(k)
    levels = np.array([10, -10, 5, -5, 0])
    if k % 512:
        return np.exp2(np.random.permutation(np.resize(levels, k // 32))).repeat(32)
    a = np.empty((k // 512, 16))
    for p in range(k // 512):
        a[p, :8] = np.random.permutation(np.resize(levels, 8))
        for g in range(8):
            far = levels[np.abs(levels - a[p, g]) >= 10]
            a[p, g + 8] = far[np.random.randint(len(far))]
    return np.exp2(a.ravel()).repeat(32)


BF16 = ml_dtypes.bfloat16


def bf(x):
    return np.asarray(x, np.float32).astype(BF16)


def f64(x):
    return np.asarray(x).astype(np.float64)


B, C, CK, H, W = 32, 512, 512, 16, 16
N = H * W


def draw0():
    s, t = mx_kscale(C), mx_kscale(CK)
    return {
        "x": bf(np.random.standard_normal((B, C, H, W)) * s[None, :, None, None]),
        "Wq": bf(np.random.standard_normal((CK, C)) / np.sqrt(C) / s[None, :] * t[:, None]),
        "bq": bf(np.random.standard_normal(CK) * 0.3 * t),
        "Wk": bf(np.random.standard_normal((CK, C)) / np.sqrt(C) / s[None, :] / t[:, None]),
        "bk": bf(np.random.standard_normal(CK) * 0.3 / t),
        "fg_sim": bf(np.random.uniform(size=(B, N, N))),
    }


def core(x, Wq, bq, Wk, bk, fg_sim):
    xq = mxq(f64(x).reshape(B, C, N), 1, "e4m3")
    query = (mxq(f64(Wq), 1, "e4m3") @ xq).transpose(0, 2, 1) + f64(bq)
    key = (mxq(f64(Wk), 1, "e4m3") @ xq) + f64(bk)[None, :, None]
    sim = (mxq(query, 2, "e4m3") @ mxq(key, 1, "e4m3")) * CK ** -0.5
    return sim * f64(fg_sim)


def e4m3fn_bytes(y):
    return np.clip(np.asarray(y, np.float64), -448.0, 448.0).astype(np.float32).astype(ml_dtypes.float8_e4m3fn).view(np.uint8)


def e4m3fn_values(b):
    return np.asarray(b, np.uint8).view(ml_dtypes.float8_e4m3fn).astype(np.float64)


def setup_inputs():
    d = draw0()
    x0 = np.asarray(d['x']).astype(np.float64)
    s = (np.max(np.abs(x0), axis=(0, 2, 3), keepdims=True) / 448.0).astype(np.float32)
    out = {}
    for k, v in d.items():
        if k == 'x':
            out['x_bytes'] = e4m3fn_bytes(x0 / s.astype(np.float64))
            out['x_scale'] = s
        else:
            out[k] = v
    return out


def reference(x_bytes, x_scale, Wq, bq, Wk, bk, fg_sim):
    return core(e4m3fn_values(x_bytes) * x_scale.astype(np.float64), Wq, bq, Wk, bk, fg_sim)

@@ -1,0 +1,205 @@
+from contextlib import ExitStack
+
+import concourse.mybir as mybir
+from concourse.masks import make_identity
+
+B, C, CK, N = 32, 512, 512, 256
+FLOPS = 2 * B * (2 * CK * C * N + N * N * CK)
+
+F32 = mybir.dt.float32
+BF16 = mybir.dt.bfloat16
+U32 = mybir.dt.uint32
+U8 = mybir.dt.uint8
+FP8 = mybir.dt.float8_e4m3fn
+FP8X4 = mybir.dt.float8_e4m3fn_x4
+ACT = mybir.ActivationFunctionType
+ALU = mybir.AluOpType
+
+P = 128
+T = 4
+GROUPS = [1] + [2] * 15 + [1]
+FIRST = [sum(GROUPS[:i]) for i in range(len(GROUPS))]
+STEPS = len(GROUPS)
+RUN = 4
+
+
+def tile_sgan_pa_t_kernel(tc, x_bytes, x_scale, Wq, bq, Wk, bk, fg_sim, out):
+    nc = tc.nc
+    with ExitStack() as ctx:
+        keep = ctx.enter_context(tc.tile_pool(name="keep", bufs=1))
+        pool = ctx.enter_context(tc.tile_pool(name="pool", bufs=3))
+        loads = ctx.enter_context(tc.tile_pool(name="loads", bufs=5))
+        psum = ctx.enter_context(tc.psum_pool(name="psum", bufs=6))
+        psim = ctx.enter_context(tc.psum_pool(name="psim", bufs=2))
+        ctx.enter_context(tc.manual_schedule())
+
+        st = {}
+
+        def load_x(i):
+            xb = loads.tile([P, T, GROUPS[i] * N], U8, name="x_codes_in", align_bytes=64)
+            for b in range(GROUPS[i]):
+                nc.sync.dma_start(
+                    out=xb[:, :, b * N : (b + 1) * N],
+                    in_=x_bytes[FIRST[i] + b].rearrange("(p t) h w -> p t (h w)", t=T),
+                )
+            st["xb", i] = xb
+
+        def load_fg(i):
+            fg = loads.tile([P, GROUPS[i] * 2, N], BF16, name="fg", align_bytes=64)
+            nc.sync.dma_start(
+                out=fg[:], in_=fg_sim[FIRST[i] : FIRST[i] + GROUPS[i]].rearrange("b (q p) m -> p (b q) m", p=P)
+            )
+            st["fg", i] = fg
+
+        xs = keep.tile([P, T], F32, name="xs")
+
+        def widen(i):
+            xp = pool.tile([P, T, GROUPS[i] * N], BF16, name="x_planes", align_bytes=64)
+            xb = st["xb", i]
+            for t in range(T):
+                nc.scalar.activation(
+                    out=xp[:, t, :], in_=xb[:, t, :].bitcast(FP8), func=ACT.Copy, scale=xs[:, t : t + 1]
+                )
+            st["xp", i] = xp
+
+        def interleave(planes, name, cols):
+            g = pool.tile([P, cols, T], BF16, name=name, align_bytes=64)
+            nc.vector.tensor_copy(
+                out=g[:].rearrange("p (c i) t -> p c t i", i=RUN),
+                in_=planes[:].rearrange("p t (c i) -> p c t i", i=RUN),
+            )
+            return g
+
+        def quantize(g, pl, name, cols):
+            codes = pl.tile([P, cols], U32, name=name + "_codes", align_bytes=64)
+            scales = pl.tile([P, cols], U8, name=name + "_scales", align_bytes=64)
+            nc.vector.quantize_mx(
+                out=codes[:].bitcast(FP8X4), scales=scales[:], in_=g[:].rearrange("p c t -> p (c t)")
+            )
+            return codes, scales
+
+        def ilv_x(i):
+            st["xg", i] = interleave(st["xp", i], "x_grouped", GROUPS[i] * N)
+
+        def quant_x(i):
+            st["xc", i] = quantize(st["xg", i], pool, "x", GROUPS[i] * N)
+
+        def mx(dst, l, ls, r, rs):
+            nc.tensor.matmul_mx(
+                out=dst, lhsT=l.bitcast(FP8X4), lhsT_scale=ls, rhs=r.bitcast(FP8X4), rhs_scale=rs, start=True, stop=True
+            )
+
+        def project(i, w, which, bias):
+            xc, xsc = st["xc", i]
+            wc, wsc = w
+            cols = GROUPS[i] * N
+            pl = pool.tile([P, T, cols], BF16, name=which + "_planes", align_bytes=64)
+            for t in range(T):
+                acc = psum.tile([P, cols], F32, name="acc")
+                ms = slice(t * P, (t + 1) * P)
+                mx(acc[:], wc[:, ms], wsc[:, ms], xc[:], xsc[:])
+                nc.scalar.activation(out=pl[:, t, :], in_=acc[:], func=ACT.Identity, bias=bias[:, t : t + 1])
+            st[which, i] = pl
+
+        def sim(i):
+            qc, qs = st["qc", i]
+            kc, ks = st["kc", i]
+            for b in range(GROUPS[i]):
+                s = psim.tile([P, 2, N], F32, name="s")
+                for nb in range(2):
+                    ms = slice(b * N + nb * P, b * N + (nb + 1) * P)
+                    ns = slice(b * N, (b + 1) * N)
+                    mx(s[:, nb, :], qc[:, ms], qs[:, ms], kc[:, ns], ks[:, ns])
+                st["s", i, b] = s
+
+        def finish(i, b):
+            if b >= GROUPS[i]:
+                return
+            o = pool.tile([P, 2, N], F32, name="o", align_bytes=64)
+            nc.vector.scalar_tensor_tensor(
+                out=o[:],
+                in0=st["s", i, b][:],
+                scalar=CK**-0.5,
+                in1=st["fg", i][:, 2 * b : 2 * b + 2, :],
+                op0=ALU.mult,
+                op1=ALU.mult,
+            )
+            nc.sync.dma_start(out=out[FIRST[i] + b].rearrange("(q p) m -> p q m", p=P), in_=o[:])
+
+        nc.sync.dma_start(out=xs[:], in_=x_scale.rearrange("a (p t) b c -> p (a t b c)", t=T))
+        load_x(0)
+        wraw = {}
+        for name, w in (("q", Wq), ("k", Wk)):
+            raw = keep.tile([P, T, C], BF16, name="w_raw_" + name, align_bytes=64)
+            nc.sync.dma_start(out=raw[:], in_=w.rearrange("(m t) k -> m t k", t=T))
+            wraw[name] = raw
+            if name == "q":
+                load_x(1)
+        biases = {}
+        for name, v in (("q", bq), ("k", bk)):
+            b16 = keep.tile([P, T], BF16, name="b16_" + name)
+            nc.sync.dma_start(out=b16[:], in_=v.rearrange("(p t) -> p t", t=T))
+            biases[name] = b16
+        for i in range(2, 3):
+            load_x(i)
+        load_fg(0)
+        load_fg(1)
+
+        ident = keep.tile([P, P], F32, name="ident")
+        make_identity(nc, ident[:])
+
+        def turn_w(name, copy):
+            words = wraw[name][:].rearrange("p t k -> p (t k)").bitcast(F32)
+            g = keep.tile([P, CK, T], BF16, name="w_grouped_" + name, align_bytes=64)
+            gw = g[:].rearrange("p c t -> p (c t)").bitcast(F32).rearrange("p (r m u) -> p r m u", r=T, u=2)
+            for h in range(2):
+                wt = psum.tile([P, 2, 2, P], F32, name="acc")
+                for r in range(2):
+                    for u in range(2):
+                        o = (2 * h + r) * (C // 2)
+                        nc.tensor.transpose(wt[:, r, u, :], words[:, o + u : o + C // 2 : 2], ident[:])
+                copy(out=gw[:, 2 * h : 2 * h + 2], in_=wt[:].rearrange("p r u m -> p r m u"))
+            return g
+
+        widen(0)
+        gq = turn_w("q", nc.vector.tensor_copy)
+        bias = {}
+        widen(1)
+        gk = turn_w("k", nc.scalar.copy)
+        ilv_x(0)
+        wq = quantize(gq, keep, "wq", CK)
+        quant_x(0)
+        for name in ("q", "k"):
+            b32 = keep.tile([P, T], F32, name="b32_" + name)
+            nc.vector.tensor_copy(out=b32[:], in_=biases[name][:])
+            bias[name] = b32
+        wk = quantize(gk, keep, "wk", CK)
+        ilv_x(1)
+
+        for i in range(STEPS + 1):
+            if i + 3 < STEPS:
+                load_x(i + 3)
+            if i + 2 < STEPS:
+                load_fg(i + 2)
+            if i < STEPS:
+                project(i, wq, "q", bias["q"])
+                project(i, wk, "k", bias["k"])
+            if i >= 1:
+                sim(i - 1)
+            if i + 2 < STEPS:
+                widen(i + 2)
+            if i < STEPS:
+                st["qg", i] = interleave(st["q", i], "q_grouped", GROUPS[i] * N)
+            if i + 1 < STEPS:
+                quant_x(i + 1)
+            if i >= 1:
+                finish(i - 1, 0)
+            if i < STEPS:
+                st["qc", i] = quantize(st["qg", i], pool, "q", GROUPS[i] * N)
+                st["kg", i] = interleave(st["k", i], "k_grouped", GROUPS[i] * N)
+            if i >= 1:
+                finish(i - 1, 1)
+            if i < STEPS:
+                st["kc", i] = quantize(st["kg", i], pool, "k", GROUPS[i] * N)
+            if i + 2 < STEPS:
+                ilv_x(i + 2)

@@ -20,15 +20,20 @@ T = 4
 GROUPS = [1] + [2] * 15 + [1]
 FIRST = [sum(GROUPS[:i]) for i in range(len(GROUPS))]
 STEPS = len(GROUPS)
-RUN = 4
+RUN = 2
+SCALAR_ILV = (16,)
+V1 = (2, 3)
+V2 = (2, 3)
+V3 = ()
+VMOD = 2
 
 
 def tile_sgan_pa_t_kernel(tc, x_bytes, x_scale, Wq, bq, Wk, bk, fg_sim, out):
     nc = tc.nc
     with ExitStack() as ctx:
         keep = ctx.enter_context(tc.tile_pool(name="keep", bufs=1))
-        pool = ctx.enter_context(tc.tile_pool(name="pool", bufs=3))
-        loads = ctx.enter_context(tc.tile_pool(name="loads", bufs=5))
+        pool = ctx.enter_context(tc.tile_pool(name="pool", bufs=4))
+        loads = ctx.enter_context(tc.tile_pool(name="loads", bufs=6))
         psum = ctx.enter_context(tc.psum_pool(name="psum", bufs=6))
         psim = ctx.enter_context(tc.psum_pool(name="psim", bufs=2))
         ctx.enter_context(tc.manual_schedule())
@@ -53,18 +58,20 @@ def tile_sgan_pa_t_kernel(tc, x_bytes, x_scale, Wq, bq, Wk, bk, fg_sim, out):
 
         xs = keep.tile([P, T], F32, name="xs")
 
-        def widen(i):
+        def widen(i, on_vector=()):
             xp = pool.tile([P, T, GROUPS[i] * N], BF16, name="x_planes", align_bytes=64)
             xb = st["xb", i]
             for t in range(T):
-                nc.scalar.activation(
-                    out=xp[:, t, :], in_=xb[:, t, :].bitcast(FP8), func=ACT.Copy, scale=xs[:, t : t + 1]
-                )
+                dst, src, scale = xp[:, t, :], xb[:, t, :].bitcast(FP8), xs[:, t : t + 1]
+                if t in on_vector:
+                    nc.vector.tensor_scalar(out=dst, in0=src, scalar1=scale, scalar2=None, op0=ALU.mult)
+                else:
+                    nc.scalar.activation(out=dst, in_=src, func=ACT.Copy, scale=scale)
             st["xp", i] = xp
 
-        def interleave(planes, name, cols):
+        def interleave(planes, name, cols, copy=nc.vector.tensor_copy):
             g = pool.tile([P, cols, T], BF16, name=name, align_bytes=64)
-            nc.vector.tensor_copy(
+            copy(
                 out=g[:].rearrange("p (c i) t -> p c t i", i=RUN),
                 in_=planes[:].rearrange("p t (c i) -> p c t i", i=RUN),
             )
@@ -79,7 +86,8 @@ def tile_sgan_pa_t_kernel(tc, x_bytes, x_scale, Wq, bq, Wk, bk, fg_sim, out):
             return codes, scales
 
         def ilv_x(i):
-            st["xg", i] = interleave(st["xp", i], "x_grouped", GROUPS[i] * N)
+            copy = nc.scalar.copy if i in SCALAR_ILV else nc.vector.tensor_copy
+            st["xg", i] = interleave(st["xp", i], "x_grouped", GROUPS[i] * N, copy)
 
         def quant_x(i):
             st["xc", i] = quantize(st["xg", i], pool, "x", GROUPS[i] * N)
@@ -126,22 +134,22 @@ def tile_sgan_pa_t_kernel(tc, x_bytes, x_scale, Wq, bq, Wk, bk, fg_sim, out):
             )
             nc.sync.dma_start(out=out[FIRST[i] + b].rearrange("(q p) m -> p q m", p=P), in_=o[:])
 
-        nc.sync.dma_start(out=xs[:], in_=x_scale.rearrange("a (p t) b c -> p (a t b c)", t=T))
         load_x(0)
+        nc.sync.dma_start(out=xs[:], in_=x_scale.rearrange("a (p t) b c -> p (a t b c)", t=T))
+        load_x(1)
         wraw = {}
         for name, w in (("q", Wq), ("k", Wk)):
             raw = keep.tile([P, T, C], BF16, name="w_raw_" + name, align_bytes=64)
             nc.sync.dma_start(out=raw[:], in_=w.rearrange("(m t) k -> m t k", t=T))
             wraw[name] = raw
             if name == "q":
-                load_x(1)
+                load_x(2)
         biases = {}
         for name, v in (("q", bq), ("k", bk)):
             b16 = keep.tile([P, T], BF16, name="b16_" + name)
             nc.sync.dma_start(out=b16[:], in_=v.rearrange("(p t) -> p t", t=T))
             biases[name] = b16
-        for i in range(2, 3):
-            load_x(i)
+        load_x(3)
         load_fg(0)
         load_fg(1)
 
@@ -161,33 +169,37 @@ def tile_sgan_pa_t_kernel(tc, x_bytes, x_scale, Wq, bq, Wk, bk, fg_sim, out):
                 copy(out=gw[:, 2 * h : 2 * h + 2], in_=wt[:].rearrange("p r u m -> p r m u"))
             return g
 
-        widen(0)
-        gq = turn_w("q", nc.vector.tensor_copy)
         bias = {}
-        widen(1)
-        gk = turn_w("k", nc.scalar.copy)
-        ilv_x(0)
-        wq = quantize(gq, keep, "wq", CK)
-        quant_x(0)
         for name in ("q", "k"):
             b32 = keep.tile([P, T], F32, name="b32_" + name)
-            nc.vector.tensor_copy(out=b32[:], in_=biases[name][:])
+            nc.gpsimd.tensor_copy(out=b32[:], in_=biases[name][:])
             bias[name] = b32
-        wk = quantize(gk, keep, "wk", CK)
+        widen(0, on_vector=range(T))
+        ilv_x(0)
+        widen(1, on_vector=V1)
+        quant_x(0)
+        gq = turn_w("q", nc.vector.tensor_copy)
+        widen(2, on_vector=V2)
+        wq = quantize(gq, keep, "wq", CK)
+        gk = turn_w("k", nc.vector.tensor_copy)
         ilv_x(1)
+        wk = quantize(gk, keep, "wk", CK)
 
         for i in range(STEPS + 1):
-            if i + 3 < STEPS:
-                load_x(i + 3)
+            if i + 4 < STEPS:
+                load_x(i + 4)
             if i + 2 < STEPS:
                 load_fg(i + 2)
             if i < STEPS:
                 project(i, wq, "q", bias["q"])
+            if i == 0:
+                widen(3, on_vector=V3)
+            if i < STEPS:
                 project(i, wk, "k", bias["k"])
             if i >= 1:
                 sim(i - 1)
-            if i + 2 < STEPS:
-                widen(i + 2)
+            if i >= 1 and i + 3 < STEPS:
+                widen(i + 3, on_vector=(3,) if (i + 3) % VMOD == 0 else ())
             if i < STEPS:
                 st["qg", i] = interleave(st["q", i], "q_grouped", GROUPS[i] * N)
             if i + 1 < STEPS:

@@ -23,9 +23,11 @@ STEPS = len(GROUPS)
 RUN = 2
 SCALAR_ILV = (16,)
 V1 = (2, 3)
-V2 = (2, 3)
-V3 = ()
-VMOD = 2
+V2 = (3,)
+V3 = (3,)
+VP = ((1, 2, 3),)
+X_FIRST = 3
+X_N = (2,)
 
 
 def tile_sgan_pa_t_kernel(tc, x_bytes, x_scale, Wq, bq, Wk, bk, fg_sim, out):
@@ -34,7 +36,8 @@ def tile_sgan_pa_t_kernel(tc, x_bytes, x_scale, Wq, bq, Wk, bk, fg_sim, out):
         keep = ctx.enter_context(tc.tile_pool(name="keep", bufs=1))
         pool = ctx.enter_context(tc.tile_pool(name="pool", bufs=4))
         loads = ctx.enter_context(tc.tile_pool(name="loads", bufs=6))
-        psum = ctx.enter_context(tc.psum_pool(name="psum", bufs=6))
+        psum = ctx.enter_context(tc.psum_pool(name="psum", bufs=5))
+        pturn = ctx.enter_context(tc.psum_pool(name="pturn", bufs=1))
         psim = ctx.enter_context(tc.psum_pool(name="psim", bufs=2))
         ctx.enter_context(tc.manual_schedule())
 
@@ -69,12 +72,15 @@ def tile_sgan_pa_t_kernel(tc, x_bytes, x_scale, Wq, bq, Wk, bk, fg_sim, out):
                     nc.scalar.activation(out=dst, in_=src, func=ACT.Copy, scale=scale)
             st["xp", i] = xp
 
-        def interleave(planes, name, cols, copy=nc.vector.tensor_copy):
-            g = pool.tile([P, cols, T], BF16, name=name, align_bytes=64)
+        def interleave(g, planes, copy):
             copy(
-                out=g[:].rearrange("p (c i) t -> p c t i", i=RUN),
-                in_=planes[:].rearrange("p t (c i) -> p c t i", i=RUN),
+                out=g.rearrange("p (c i) t -> p c t i", i=RUN),
+                in_=planes.rearrange("p t (c i) -> p c t i", i=RUN),
             )
+
+        def grouped(i, which):
+            g = pool.tile([P, GROUPS[i] * N, T], BF16, name=which + "_grouped", align_bytes=64)
+            interleave(g[:], st[which, i][:], nc.vector.tensor_copy)
             return g
 
         def quantize(g, pl, name, cols):
@@ -86,8 +92,29 @@ def tile_sgan_pa_t_kernel(tc, x_bytes, x_scale, Wq, bq, Wk, bk, fg_sim, out):
             return codes, scales
 
         def ilv_x(i):
+            if turned(i):
+                if turned(i) == 1:
+                    interleave(st["xg", i][:, N:, :], st["xp", i][:, :, N:], nc.vector.tensor_copy)
+                return
+            st["xg", i] = pool.tile([P, GROUPS[i] * N, T], BF16, name="x_grouped", align_bytes=64)
             copy = nc.scalar.copy if i in SCALAR_ILV else nc.vector.tensor_copy
-            st["xg", i] = interleave(st["xp", i], "x_grouped", GROUPS[i] * N, copy)
+            interleave(st["xg", i][:], st["xp", i][:], copy)
+
+        def turned(i):
+            return X_N[i % len(X_N)] if X_FIRST <= i < STEPS and GROUPS[i] == 2 else 0
+
+        def turn_x(i, b):
+            xt = pturn.tile([P, N, T], BF16, name="xt")
+            for h in range(2):
+                ns = slice(h * P, (h + 1) * P)
+                src = st["xp", i][:, :, b * N + h * P : b * N + (h + 1) * P].rearrange("p t n -> p n t")
+                nc.tensor.matmul(xt[:, ns, :], lhsT=ident16[:], rhs=src, start=True, stop=True)
+            st["xt", i] = xt
+
+        def take_x(i, b):
+            if b == 0:
+                st["xg", i] = pool.tile([P, GROUPS[i] * N, T], BF16, name="x_grouped", align_bytes=64)
+            nc.scalar.copy(out=st["xg", i][:, b * N : (b + 1) * N, :], in_=st["xt", i][:])
 
         def quant_x(i):
             st["xc", i] = quantize(st["xg", i], pool, "x", GROUPS[i] * N)
@@ -97,17 +124,20 @@ def tile_sgan_pa_t_kernel(tc, x_bytes, x_scale, Wq, bq, Wk, bk, fg_sim, out):
                 out=dst, lhsT=l.bitcast(FP8X4), lhsT_scale=ls, rhs=r.bitcast(FP8X4), rhs_scale=rs, start=True, stop=True
             )
 
-        def project(i, w, which, bias):
+        def plane_mm(i, w, which, t):
             xc, xsc = st["xc", i]
             wc, wsc = w
-            cols = GROUPS[i] * N
-            pl = pool.tile([P, T, cols], BF16, name=which + "_planes", align_bytes=64)
-            for t in range(T):
-                acc = psum.tile([P, cols], F32, name="acc")
-                ms = slice(t * P, (t + 1) * P)
-                mx(acc[:], wc[:, ms], wsc[:, ms], xc[:], xsc[:])
-                nc.scalar.activation(out=pl[:, t, :], in_=acc[:], func=ACT.Identity, bias=bias[:, t : t + 1])
-            st[which, i] = pl
+            acc = psum.tile([P, GROUPS[i] * N], F32, name="acc")
+            ms = slice(t * P, (t + 1) * P)
+            mx(acc[:], wc[:, ms], wsc[:, ms], xc[:], xsc[:])
+            st[which, i, t] = acc
+
+        def plane_ev(i, which, t):
+            if t == 0:
+                st[which, i] = pool.tile([P, T, GROUPS[i] * N], BF16, name=which + "_planes", align_bytes=64)
+            nc.scalar.activation(
+                out=st[which, i][:, t, :], in_=st[which, i, t][:], func=ACT.Identity, bias=bias[which][:, t : t + 1]
+            )
 
         def sim(i):
             qc, qs = st["qc", i]
@@ -155,6 +185,8 @@ def tile_sgan_pa_t_kernel(tc, x_bytes, x_scale, Wq, bq, Wk, bk, fg_sim, out):
 
         ident = keep.tile([P, P], F32, name="ident")
         make_identity(nc, ident[:])
+        ident16 = keep.tile([P, P], BF16, name="ident16")
+        make_identity(nc, ident16[:])
 
         def turn_w(name, copy):
             words = wraw[name][:].rearrange("p t k -> p (t k)").bitcast(F32)
@@ -182,8 +214,9 @@ def tile_sgan_pa_t_kernel(tc, x_bytes, x_scale, Wq, bq, Wk, bk, fg_sim, out):
         widen(2, on_vector=V2)
         wq = quantize(gq, keep, "wq", CK)
         gk = turn_w("k", nc.vector.tensor_copy)
-        ilv_x(1)
+        widen(3, on_vector=V3)
         wk = quantize(gk, keep, "wk", CK)
+        ilv_x(1)
 
         for i in range(STEPS + 1):
             if i + 4 < STEPS:
@@ -191,24 +224,37 @@ def tile_sgan_pa_t_kernel(tc, x_bytes, x_scale, Wq, bq, Wk, bk, fg_sim, out):
             if i + 2 < STEPS:
                 load_fg(i + 2)
             if i < STEPS:
-                project(i, wq, "q", bias["q"])
-            if i == 0:
-                widen(3, on_vector=V3)
+                for t in range(T):
+                    plane_mm(i, wq, "q", t)
+                    plane_ev(i, "q", t)
+                plane_mm(i, wk, "k", 0)
+            tx = turned(i + 2) if i + 2 < STEPS else 0
+            if tx:
+                turn_x(i + 2, 0)
+            if tx == 2:
+                take_x(i + 2, 0)
             if i < STEPS:
-                project(i, wk, "k", bias["k"])
+                for t in range(T):
+                    if t:
+                        plane_mm(i, wk, "k", t)
+                    plane_ev(i, "k", t)
             if i >= 1:
                 sim(i - 1)
+            if tx == 2:
+                turn_x(i + 2, 1)
+            if tx:
+                take_x(i + 2, tx - 1)
             if i >= 1 and i + 3 < STEPS:
-                widen(i + 3, on_vector=(3,) if (i + 3) % VMOD == 0 else ())
-            if i < STEPS:
-                st["qg", i] = interleave(st["q", i], "q_grouped", GROUPS[i] * N)
+                widen(i + 3, on_vector=VP[(i + 3) % len(VP)])
             if i + 1 < STEPS:
                 quant_x(i + 1)
+            if i < STEPS:
+                st["qg", i] = grouped(i, "q")
             if i >= 1:
                 finish(i - 1, 0)
             if i < STEPS:
                 st["qc", i] = quantize(st["qg", i], pool, "q", GROUPS[i] * N)
-                st["kg", i] = interleave(st["k", i], "k_grouped", GROUPS[i] * N)
+                st["kg", i] = grouped(i, "k")
             if i >= 1:
                 finish(i - 1, 1)
             if i < STEPS:

from contextlib import ExitStack

import concourse.mybir as mybir
from concourse.masks import make_identity

B, C, CK, N = 32, 512, 512, 256
FLOPS = 2 * B * (2 * CK * C * N + N * N * CK)

F32 = mybir.dt.float32
BF16 = mybir.dt.bfloat16
U32 = mybir.dt.uint32
U8 = mybir.dt.uint8
FP8 = mybir.dt.float8_e4m3fn
FP8X4 = mybir.dt.float8_e4m3fn_x4
ACT = mybir.ActivationFunctionType
ALU = mybir.AluOpType

P = 128
T = 4
GROUPS = [1] + [2] * 15 + [1]
FIRST = [sum(GROUPS[:i]) for i in range(len(GROUPS))]
STEPS = len(GROUPS)
RUN = 2
SCALAR_ILV = (16,)
V1 = (2, 3)
V2 = (3,)
V3 = (3,)
VP = ((1, 2, 3),)
X_FIRST = 3
X_N = (2,)


def tile_sgan_pa_t_kernel(tc, x_bytes, x_scale, Wq, bq, Wk, bk, fg_sim, out):
    nc = tc.nc
    with ExitStack() as ctx:
        keep = ctx.enter_context(tc.tile_pool(name="keep", bufs=1))
        pool = ctx.enter_context(tc.tile_pool(name="pool", bufs=4))
        loads = ctx.enter_context(tc.tile_pool(name="loads", bufs=6))
        psum = ctx.enter_context(tc.psum_pool(name="psum", bufs=5))
        pturn = ctx.enter_context(tc.psum_pool(name="pturn", bufs=1))
        psim = ctx.enter_context(tc.psum_pool(name="psim", bufs=2))
        ctx.enter_context(tc.manual_schedule())

        st = {}

        def load_x(i):
            xb = loads.tile([P, T, GROUPS[i] * N], U8, name="x_codes_in", align_bytes=64)
            for b in range(GROUPS[i]):
                nc.sync.dma_start(
                    out=xb[:, :, b * N : (b + 1) * N],
                    in_=x_bytes[FIRST[i] + b].rearrange("(p t) h w -> p t (h w)", t=T),
                )
            st["xb", i] = xb

        def load_fg(i):
            fg = loads.tile([P, GROUPS[i] * 2, N], BF16, name="fg", align_bytes=64)
            nc.sync.dma_start(
                out=fg[:], in_=fg_sim[FIRST[i] : FIRST[i] + GROUPS[i]].rearrange("b (q p) m -> p (b q) m", p=P)
            )
            st["fg", i] = fg

        xs = keep.tile([P, T], F32, name="xs")

        def widen(i, on_vector=()):
            xp = pool.tile([P, T, GROUPS[i] * N], BF16, name="x_planes", align_bytes=64)
            xb = st["xb", i]
            for t in range(T):
                dst, src, scale = xp[:, t, :], xb[:, t, :].bitcast(FP8), xs[:, t : t + 1]
                if t in on_vector:
                    nc.vector.tensor_scalar(out=dst, in0=src, scalar1=scale, scalar2=None, op0=ALU.mult)
                else:
                    nc.scalar.activation(out=dst, in_=src, func=ACT.Copy, scale=scale)
            st["xp", i] = xp

        def interleave(g, planes, copy):
            copy(
                out=g.rearrange("p (c i) t -> p c t i", i=RUN),
                in_=planes.rearrange("p t (c i) -> p c t i", i=RUN),
            )

        def grouped(i, which):
            g = pool.tile([P, GROUPS[i] * N, T], BF16, name=which + "_grouped", align_bytes=64)
            interleave(g[:], st[which, i][:], nc.vector.tensor_copy)
            return g

        def quantize(g, pl, name, cols):
            codes = pl.tile([P, cols], U32, name=name + "_codes", align_bytes=64)
            scales = pl.tile([P, cols], U8, name=name + "_scales", align_bytes=64)
            nc.vector.quantize_mx(
                out=codes[:].bitcast(FP8X4), scales=scales[:], in_=g[:].rearrange("p c t -> p (c t)")
            )
            return codes, scales

        def ilv_x(i):
            if turned(i):
                if turned(i) == 1:
                    interleave(st["xg", i][:, N:, :], st["xp", i][:, :, N:], nc.vector.tensor_copy)
                return
            st["xg", i] = pool.tile([P, GROUPS[i] * N, T], BF16, name="x_grouped", align_bytes=64)
            copy = nc.scalar.copy if i in SCALAR_ILV else nc.vector.tensor_copy
            interleave(st["xg", i][:], st["xp", i][:], copy)

        def turned(i):
            return X_N[i % len(X_N)] if X_FIRST <= i < STEPS and GROUPS[i] == 2 else 0

        def turn_x(i, b):
            xt = pturn.tile([P, N, T], BF16, name="xt")
            for h in range(2):
                ns = slice(h * P, (h + 1) * P)
                src = st["xp", i][:, :, b * N + h * P : b * N + (h + 1) * P].rearrange("p t n -> p n t")
                nc.tensor.matmul(xt[:, ns, :], lhsT=ident16[:], rhs=src, start=True, stop=True)
            st["xt", i] = xt

        def take_x(i, b):
            if b == 0:
                st["xg", i] = pool.tile([P, GROUPS[i] * N, T], BF16, name="x_grouped", align_bytes=64)
            nc.scalar.copy(out=st["xg", i][:, b * N : (b + 1) * N, :], in_=st["xt", i][:])

        def quant_x(i):
            st["xc", i] = quantize(st["xg", i], pool, "x", GROUPS[i] * N)

        def mx(dst, l, ls, r, rs):
            nc.tensor.matmul_mx(
                out=dst, lhsT=l.bitcast(FP8X4), lhsT_scale=ls, rhs=r.bitcast(FP8X4), rhs_scale=rs, start=True, stop=True
            )

        def plane_mm(i, w, which, t):
            xc, xsc = st["xc", i]
            wc, wsc = w
            acc = psum.tile([P, GROUPS[i] * N], F32, name="acc")
            ms = slice(t * P, (t + 1) * P)
            mx(acc[:], wc[:, ms], wsc[:, ms], xc[:], xsc[:])
            st[which, i, t] = acc

        def plane_ev(i, which, t):
            if t == 0:
                st[which, i] = pool.tile([P, T, GROUPS[i] * N], BF16, name=which + "_planes", align_bytes=64)
            nc.scalar.activation(
                out=st[which, i][:, t, :], in_=st[which, i, t][:], func=ACT.Identity, bias=bias[which][:, t : t + 1]
            )

        def sim(i):
            qc, qs = st["qc", i]
            kc, ks = st["kc", i]
            for b in range(GROUPS[i]):
                s = psim.tile([P, 2, N], F32, name="s")
                for nb in range(2):
                    ms = slice(b * N + nb * P, b * N + (nb + 1) * P)
                    ns = slice(b * N, (b + 1) * N)
                    mx(s[:, nb, :], qc[:, ms], qs[:, ms], kc[:, ns], ks[:, ns])
                st["s", i, b] = s

        def finish(i, b):
            if b >= GROUPS[i]:
                return
            o = pool.tile([P, 2, N], F32, name="o", align_bytes=64)
            nc.vector.scalar_tensor_tensor(
                out=o[:],
                in0=st["s", i, b][:],
                scalar=CK**-0.5,
                in1=st["fg", i][:, 2 * b : 2 * b + 2, :],
                op0=ALU.mult,
                op1=ALU.mult,
            )
            nc.sync.dma_start(out=out[FIRST[i] + b].rearrange("(q p) m -> p q m", p=P), in_=o[:])

        load_x(0)
        nc.sync.dma_start(out=xs[:], in_=x_scale.rearrange("a (p t) b c -> p (a t b c)", t=T))
        load_x(1)
        wraw = {}
        for name, w in (("q", Wq), ("k", Wk)):
            raw = keep.tile([P, T, C], BF16, name="w_raw_" + name, align_bytes=64)
            nc.sync.dma_start(out=raw[:], in_=w.rearrange("(m t) k -> m t k", t=T))
            wraw[name] = raw
            if name == "q":
                load_x(2)
        biases = {}
        for name, v in (("q", bq), ("k", bk)):
            b16 = keep.tile([P, T], BF16, name="b16_" + name)
            nc.sync.dma_start(out=b16[:], in_=v.rearrange("(p t) -> p t", t=T))
            biases[name] = b16
        load_x(3)
        load_fg(0)
        load_fg(1)

        ident = keep.tile([P, P], F32, name="ident")
        make_identity(nc, ident[:])
        ident16 = keep.tile([P, P], BF16, name="ident16")
        make_identity(nc, ident16[:])

        def turn_w(name, copy):
            words = wraw[name][:].rearrange("p t k -> p (t k)").bitcast(F32)
            g = keep.tile([P, CK, T], BF16, name="w_grouped_" + name, align_bytes=64)
            gw = g[:].rearrange("p c t -> p (c t)").bitcast(F32).rearrange("p (r m u) -> p r m u", r=T, u=2)
            for h in range(2):
                wt = psum.tile([P, 2, 2, P], F32, name="acc")
                for r in range(2):
                    for u in range(2):
                        o = (2 * h + r) * (C // 2)
                        nc.tensor.transpose(wt[:, r, u, :], words[:, o + u : o + C // 2 : 2], ident[:])
                copy(out=gw[:, 2 * h : 2 * h + 2], in_=wt[:].rearrange("p r u m -> p r m u"))
            return g

        bias = {}
        for name in ("q", "k"):
            b32 = keep.tile([P, T], F32, name="b32_" + name)
            nc.gpsimd.tensor_copy(out=b32[:], in_=biases[name][:])
            bias[name] = b32
        widen(0, on_vector=range(T))
        ilv_x(0)
        widen(1, on_vector=V1)
        quant_x(0)
        gq = turn_w("q", nc.vector.tensor_copy)
        widen(2, on_vector=V2)
        wq = quantize(gq, keep, "wq", CK)
        gk = turn_w("k", nc.vector.tensor_copy)
        widen(3, on_vector=V3)
        wk = quantize(gk, keep, "wk", CK)
        ilv_x(1)

        for i in range(STEPS + 1):
            if i + 4 < STEPS:
                load_x(i + 4)
            if i + 2 < STEPS:
                load_fg(i + 2)
            if i < STEPS:
                for t in range(T):
                    plane_mm(i, wq, "q", t)
                    plane_ev(i, "q", t)
                plane_mm(i, wk, "k", 0)
            tx = turned(i + 2) if i + 2 < STEPS else 0
            if tx:
                turn_x(i + 2, 0)
            if tx == 2:
                take_x(i + 2, 0)
            if i < STEPS:
                for t in range(T):
                    if t:
                        plane_mm(i, wk, "k", t)
                    plane_ev(i, "k", t)
            if i >= 1:
                sim(i - 1)
            if tx == 2:
                turn_x(i + 2, 1)
            if tx:
                take_x(i + 2, tx - 1)
            if i >= 1 and i + 3 < STEPS:
                widen(i + 3, on_vector=VP[(i + 3) % len(VP)])
            if i + 1 < STEPS:
                quant_x(i + 1)
            if i < STEPS:
                st["qg", i] = grouped(i, "q")
            if i >= 1:
                finish(i - 1, 0)
            if i < STEPS:
                st["qc", i] = quantize(st["qg", i], pool, "q", GROUPS[i] * N)
                st["kg", i] = grouped(i, "k")
            if i >= 1:
                finish(i - 1, 1)
            if i < STEPS:
                st["kc", i] = quantize(st["kg", i], pool, "k", GROUPS[i] * N)
            if i + 2 < STEPS:
                ilv_x(i + 2)
